import numpy as np
import ml_dtypes


def mxq(x, axis, fmt="e4m3"):
    dtype, down = {"e4m3": (ml_dtypes.float8_e4m3fn, 7), "e5m2": (ml_dtypes.float8_e5m2, 14)}[fmt]
    v = np.moveaxis(np.asarray(x, np.float32).astype(ml_dtypes.bfloat16).astype(np.float64), axis, -1)
    blocks = v.reshape(v.shape[:-1] + (-1, 32))
    amax = np.abs(blocks).max(-1, keepdims=True)
    byte = np.maximum(np.where(amax > 0, np.frexp(amax)[1] - 1 + 127, 0) - down, 1)
    scale = np.exp2(byte - 127.0)
    codes = (blocks / scale).astype(np.float32).astype(dtype).astype(np.float64)
    return np.moveaxis((codes * scale).reshape(v.shape), -1, axis)


WIDE = False


def mx_kscale(k):
    if not WIDE:
        return np.ones(k)
    levels = np.array([30, -30])
    if k % 512:
        return np.exp2(np.random.permutation(np.resize(levels, k // 32))).repeat(32)
    a = np.empty((k // 512, 16))
    for p in range(k // 512):
        a[p, :8] = np.random.permutation(np.resize(levels, 8))
        for g in range(8):
            far = levels[np.abs(levels - a[p, g]) >= 10]
            a[p, g + 8] = far[np.random.randint(len(far))]
    return np.exp2(a.ravel()).repeat(32)


BF16 = ml_dtypes.bfloat16


def bf(x):
    return np.asarray(x, np.float32).astype(BF16)


def f64(x):
    return np.asarray(x).astype(np.float64)


B, N, F, D, DIM = 2, 512, 512, 2048, 32
EPS = 1e-6
RAD = 3.0


def expmap0_full(us):
    r = np.sqrt((us * us).sum(-1, keepdims=True))
    rs = np.maximum(r, EPS)
    x0 = 0.5 * (np.exp(r) + np.exp(-r))
    xs = (0.5 * (np.exp(rs) - np.exp(-rs)) / rs) * us
    return np.concatenate([x0, xs], axis=-1)


def setup_inputs():
    s = mx_kscale(F)
    amp = 0.5 + 0.5 * np.random.random((B, N, 1))
    return {"x": bf(np.random.standard_normal((B, N, F)) * amp * s),
            "w_sp": bf(np.random.standard_normal((F, D)) * RAD / np.sqrt(D * F) / s[:, None])}


def reference(x, w_sp):
    us = mxq(f64(x), 2, "e5m2") @ mxq(f64(w_sp), 0, "e4m3")
    return expmap0_full(us)

@@ -1,0 +1,271 @@
+import math
+from contextlib import ExitStack
+
+import concourse.mybir as mybir
+from concourse.masks import make_identity
+
+B, N, F, D = 2, 512, 512, 2048
+EPS = 1e-6
+SINH_EPS = EPS + EPS**3 / 6
+FLOPS = 2 * B * N * F * D
+
+F32 = mybir.dt.float32
+BF16 = mybir.dt.bfloat16
+U32 = mybir.dt.uint32
+U8 = mybir.dt.uint8
+E5M2X4 = mybir.dt.float8_e5m2_x4
+E4M3X4 = mybir.dt.float8_e4m3fn_x4
+ALU = mybir.AluOpType
+ACT = mybir.ActivationFunctionType
+
+P = 128
+PACK = 4
+TILES = B * N // P
+BANK = 512
+CHUNKS = D // BANK
+ROW = D + 1
+PAIR = 2
+RUN = 4
+SCALAR_COLS = (256, 256, 256, 0)
+
+
+def tile_hgcn_pb_kernel(tc, x, w_sp, out):
+    nc = tc.nc
+    x_rows = x.rearrange("b (q j) f -> (b q) j f", j=TILES)
+    w_rows = w_sp.rearrange("(p t) d -> p t d", t=PACK)
+    out_rows = out.rearrange("b (q j) d -> (b q) (j d)", j=TILES)
+
+    with ExitStack() as ctx:
+        keep = ctx.enter_context(tc.tile_pool(name="keep", bufs=1))
+        waste = ctx.enter_context(tc.tile_pool(name="waste", bufs=4))
+        psum = ctx.enter_context(tc.psum_pool(name="psum", bufs=1))
+        ctx.enter_context(tc.manual_schedule())
+
+        def new(name, shape, dtype):
+            return keep.tile(shape, dtype, name=name, align_bytes=64)
+
+        w_raw = [new(f"w_raw{c}", [P, PACK, BANK], BF16) for c in range(CHUNKS)]
+        w_grouped = [new(f"w_grouped{c}", [P, BANK, PACK], BF16) for c in range(CHUNKS)]
+        w_codes = [new(f"w_codes{c}", [P, BANK], U32) for c in range(CHUNKS)]
+        w_scales = [new(f"w_scales{c}", [P, BANK], U8) for c in range(CHUNKS)]
+        pairs = TILES // PAIR
+        x_raw = [new(f"x_raw{g}", [P, PAIR, F], BF16) for g in range(pairs)]
+        x_grouped = [new(f"x_grouped{g}", [P, PAIR * P * PACK], BF16) for g in range(pairs)]
+        x_codes = [new(f"x_codes{g}", [P, PAIR * P], U32) for g in range(pairs)]
+        x_scales = [new(f"x_scales{g}", [P, PAIR * P], U8) for g in range(pairs)]
+        result = new("result", [P, TILES * ROW], F32)
+        identity = new("identity", [P, P], F32)
+        signs = new("signs", [P, 2], F32)
+        half = new("half", [P, 1], F32)
+        neg_ln2 = new("neg_ln2", [P, 1], F32)
+
+        def load_w(c, lo=0, hi=BANK):
+            nc.sync.dma_start(out=w_raw[c][:, :, lo:hi], in_=w_rows[:, :, c * BANK + lo : c * BANK + hi])
+
+        def load_x(g):
+            nc.sync.dma_start(out=x_raw[g][:], in_=x_rows[:, g * PAIR : (g + 1) * PAIR, :])
+
+        load_w(0, 0, BANK // 2)
+        load_w(0, BANK // 2, BANK)
+        load_w(1)
+        load_x(0)
+        for c in range(2, CHUNKS):
+            load_w(c)
+        for g in range(1, pairs):
+            load_x(g)
+
+        nc.gpsimd.memset(signs[:, 0:1], 1.0)
+        nc.gpsimd.memset(signs[:, 1:2], -1.0)
+        nc.gpsimd.memset(half[:], 0.5)
+        make_identity(nc, identity[:])
+        nc.scalar.activation(out=neg_ln2[:], in_=signs[:, 1:2], func=ACT.Identity, scale=math.log(2.0))
+
+        def interleave(copy, c, lo, hi):
+            copy(
+                out=w_grouped[c][:, lo:hi, :].rearrange("p (n i) t -> p n t i", i=RUN),
+                in_=w_raw[c][:, :, lo:hi].rearrange("p t (n i) -> p n t i", i=RUN),
+            )
+
+        def interleave_scalar(c):
+            interleave(nc.scalar.copy, c, BANK - SCALAR_COLS[c], BANK)
+
+        def interleave_vector(c):
+            interleave(nc.vector.tensor_copy, c, 0, BANK - SCALAR_COLS[c])
+
+        def quantize_w(c):
+            nc.vector.quantize_mx(
+                out=w_codes[c][:].bitcast(E4M3X4),
+                scales=w_scales[c][:],
+                in_=w_grouped[c][:].rearrange("p n t -> p (n t)"),
+            )
+
+        x_banks = {}
+
+        def transpose_x(g):
+            bank = psum.tile([P, BANK], F32, name=f"x_bank{g}", tag=f"bank{CHUNKS + g}")
+            x_banks[g] = bank
+            for i in range(PAIR):
+                words = x_raw[g][:, i, :].bitcast(F32)
+                for u in range(2):
+                    at = (2 * i + u) * P
+                    nc.tensor.transpose(bank[:, at : at + P], words[:, u :: 2], identity[:])
+
+        def unload_x(copy, g):
+            copy(
+                out=x_grouped[g][:].bitcast(F32).rearrange("p (i r u) -> p i r u", i=PAIR, u=2),
+                in_=x_banks[g][:].rearrange("p (i u r) -> p i r u", i=PAIR, u=2),
+            )
+
+        def quantize_x(g):
+            nc.vector.quantize_mx(out=x_codes[g][:].bitcast(E5M2X4), scales=x_scales[g][:], in_=x_grouped[g][:])
+
+        sums = {}
+
+        def multiply(j, c):
+            bank = psum.tile([P, BANK], F32, name=f"us{j}_{c}", tag=f"bank{CHUNKS * (j % 2) + c}")
+            sums[j, c] = bank
+            g, i = divmod(j, PAIR)
+            tokens = slice(i * P, (i + 1) * P)
+            nc.tensor.matmul_mx(
+                out=bank[:],
+                lhsT=x_codes[g][:, tokens].bitcast(E5M2X4),
+                lhsT_scale=x_scales[g][:, tokens],
+                rhs=w_codes[c][:].bitcast(E4M3X4),
+                rhs_scale=w_scales[c][:],
+                start=True,
+                stop=True,
+            )
+
+        parts = [new(f"parts{j}", [P, CHUNKS], F32) for j in range(TILES)]
+        norm = [new(f"norm{j}", [P, 4], F32) for j in range(TILES)]
+        curve = [new(f"curve{j}", [P, 3], F32) for j in range(TILES)]
+        factor = [new(f"factor{j}", [P, 4], F32) for j in range(TILES)]
+
+        def square(j, c):
+            squares = waste.tile([P, BANK], F32, name="squares")
+            nc.scalar.activation(out=squares[:], in_=sums[j, c][:], func=ACT.Square, accum_out=parts[j][:, c : c + 1])
+
+        def partial_sum(j):
+            nc.gpsimd.tensor_scalar(
+                out=norm[j][:, 0:1], in0=parts[j][:, 0:1], scalar1=parts[j][:, 1:2], scalar2=parts[j][:, 2:3],
+                op0=ALU.add, op1=ALU.add,
+            )
+
+        def radius(j):
+            nc.gpsimd.tensor_tensor(out=norm[j][:, 1:2], in0=parts[j][:, 3:4], in1=norm[j][:, 0:1], op=ALU.add)
+            nc.gpsimd.tensor_tensor(out=norm[j][:, 2:3], in0=norm[j][:, 1:2], in1=half[:], op=ALU.pow)
+            nc.gpsimd.tensor_scalar(
+                out=norm[j][:, 3:4], in0=norm[j][:, 2:3], scalar1=EPS, scalar2=None, op0=ALU.max
+            )
+
+        def time_coordinate(j):
+            return result[:, j * ROW : j * ROW + 1]
+
+        def hyperbolics(j):
+            r = norm[j][:, 2:3]
+            nc.scalar.activation(
+                out=curve[j][:, 0:2], in_=signs[:], func=ACT.Exp, scale=r, bias=neg_ln2[:], accum_out=time_coordinate(j)
+            )
+            nc.scalar.activation(out=curve[j][:, 2:3], in_=r, func=ACT.Tanh)
+
+        def invert_radius(j):
+            nc.vector.reciprocal(out=factor[j][:, 1:2], in_=norm[j][:, 3:4])
+
+        def make_sinh(j):
+            nc.vector.tensor_scalar(
+                out=factor[j][:, 2:3], in0=curve[j][:, 2:3], scalar1=time_coordinate(j), scalar2=SINH_EPS,
+                op0=ALU.mult, op1=ALU.max,
+            )
+
+        def make_factor(j):
+            nc.vector.tensor_tensor(out=factor[j][:, 3:4], in0=factor[j][:, 1:2], in1=factor[j][:, 2:3], op=ALU.mult)
+
+        def spatial(j, c):
+            at = j * ROW + 1 + c * BANK
+            return result[:, at : at + BANK]
+
+        def scale_vector(j, c):
+            nc.vector.tensor_scalar(
+                out=spatial(j, c), in0=sums[j, c][:], scalar1=factor[j][:, 1:2], scalar2=factor[j][:, 2:3],
+                op0=ALU.mult, op1=ALU.mult,
+            )
+
+        def scale_scalar(j, c):
+            nc.scalar.activation(out=spatial(j, c), in_=sums[j, c][:], func=ACT.Copy, scale=factor[j][:, 3:4])
+
+        def store(j, c_lo, c_hi):
+            lo = j * D + c_lo * BANK
+            hi = j * D + c_hi * BANK
+            if (j, c_hi) == (TILES - 1, CHUNKS):
+                hi = TILES * ROW
+            nc.sync.dma_start(out=out_rows[:, lo:hi], in_=result[:, lo:hi])
+
+        interleave_vector(0)
+        interleave_scalar(0)
+        interleave_vector(1)
+        quantize_w(0)
+        interleave_scalar(1)
+        transpose_x(0)
+        unload_x(nc.scalar.copy, 0)
+        interleave_vector(2)
+        quantize_w(1)
+        quantize_x(0)
+        interleave_scalar(2)
+        interleave_vector(3)
+        quantize_w(2)
+        quantize_w(3)
+        for c in range(CHUNKS - 1):
+            multiply(0, c)
+            square(0, c)
+        partial_sum(0)
+        multiply(1, 0)
+        transpose_x(1)
+        multiply(0, CHUNKS - 1)
+        square(0, CHUNKS - 1)
+        radius(0)
+        for g in range(2, pairs):
+            transpose_x(g)
+        for g in range(1, pairs):
+            unload_x(nc.vector.tensor_copy, g)
+            multiply(1, g)
+        for g in range(1, pairs):
+            quantize_x(g)
+
+        last = TILES - 1
+        for j in range(TILES):
+            if j < last:
+                square(j + 1, 0)
+                square(j + 1, 1)
+            else:
+                scale_scalar(j - 1, CHUNKS - 1)
+                store(j - 1, 2, CHUNKS)
+            invert_radius(j)
+            hyperbolics(j)
+            make_sinh(j)
+            if j == last:
+                make_factor(j)
+                for c in range(2):
+                    scale_vector(j, c)
+                    scale_scalar(j, c + 2)
+                    store(j, c, c + 1)
+                store(j, 2, 3)
+                store(j, 3, 4)
+                continue
+            for c in range(CHUNKS):
+                if c == 0:
+                    square(j + 1, 2)
+                    partial_sum(j + 1)
+                if c == 1:
+                    square(j + 1, 3)
+                    radius(j + 1)
+                if (j, c) == (last - 1, CHUNKS - 1):
+                    continue
+                scale_vector(j, c)
+                if (j, c) == (last - 1, 0):
+                    make_factor(j)
+                if j + 2 < TILES:
+                    multiply(j + 2, c)
+                if j == 0:
+                    store(j, c, c + 1)
+                elif c % 2 == 1:
+                    store(j, c - 1, c + 1)

@@ -26,7 +26,9 @@ CHUNKS = D // BANK
 ROW = D + 1
 PAIR = 2
 RUN = 4
-SCALAR_COLS = (256, 256, 256, 0)
+SCALAR_COLS = (0, 512, 128, 0)
+ROTATE = 1
+HYP = 1
 
 
 def tile_hgcn_pb_kernel(tc, x, w_sp, out):
@@ -38,7 +40,7 @@ def tile_hgcn_pb_kernel(tc, x, w_sp, out):
     with ExitStack() as ctx:
         keep = ctx.enter_context(tc.tile_pool(name="keep", bufs=1))
         waste = ctx.enter_context(tc.tile_pool(name="waste", bufs=4))
-        psum = ctx.enter_context(tc.psum_pool(name="psum", bufs=1))
+        psum = ctx.enter_context(tc.psum_pool(name="psum", bufs=CHUNKS))
         ctx.enter_context(tc.manual_schedule())
 
         def new(name, shape, dtype):
@@ -65,10 +67,10 @@ def tile_hgcn_pb_kernel(tc, x, w_sp, out):
         def load_x(g):
             nc.sync.dma_start(out=x_raw[g][:], in_=x_rows[:, g * PAIR : (g + 1) * PAIR, :])
 
-        load_w(0, 0, BANK // 2)
-        load_w(0, BANK // 2, BANK)
-        load_w(1)
         load_x(0)
+        for c in range(2):
+            load_w(c, 0, BANK // 2)
+            load_w(c, BANK // 2, BANK)
         for c in range(2, CHUNKS):
             load_w(c)
         for g in range(1, pairs):
@@ -92,6 +94,16 @@ def tile_hgcn_pb_kernel(tc, x, w_sp, out):
         def interleave_vector(c):
             interleave(nc.vector.tensor_copy, c, 0, BANK - SCALAR_COLS[c])
 
+        def step_square(n):
+            j, c = square_order[n]
+            square(j, c)
+            if n + CHUNKS < len(square_order):
+                multiply(to_square, *square_order[n + CHUNKS])
+            if c == CHUNKS - 2:
+                partial_sum(j)
+            if c == CHUNKS - 1:
+                radius(j)
+
         def quantize_w(c):
             nc.vector.quantize_mx(
                 out=w_codes[c][:].bitcast(E4M3X4),
@@ -102,7 +114,7 @@ def tile_hgcn_pb_kernel(tc, x, w_sp, out):
         x_banks = {}
 
         def transpose_x(g):
-            bank = psum.tile([P, BANK], F32, name=f"x_bank{g}", tag=f"bank{CHUNKS + g}")
+            bank = psum.tile([P, BANK], F32, name=f"x_bank{g}", tag="scale_banks")
             x_banks[g] = bank
             for i in range(PAIR):
                 words = x_raw[g][:, i, :].bitcast(F32)
@@ -119,10 +131,11 @@ def tile_hgcn_pb_kernel(tc, x, w_sp, out):
         def quantize_x(g):
             nc.vector.quantize_mx(out=x_codes[g][:].bitcast(E5M2X4), scales=x_scales[g][:], in_=x_grouped[g][:])
 
-        sums = {}
+        to_square, to_scale = {}, {}
 
-        def multiply(j, c):
-            bank = psum.tile([P, BANK], F32, name=f"us{j}_{c}", tag=f"bank{CHUNKS * (j % 2) + c}")
+        def multiply(sums, j, c):
+            tag = "square_banks" if sums is to_square else "scale_banks"
+            bank = psum.tile([P, BANK], F32, name=f"{tag}_{j}_{c}", tag=tag)
             sums[j, c] = bank
             g, i = divmod(j, PAIR)
             tokens = slice(i * P, (i + 1) * P)
@@ -136,6 +149,9 @@ def tile_hgcn_pb_kernel(tc, x, w_sp, out):
                 stop=True,
             )
 
+        def hold(j, c):
+            to_scale[j, c] = to_square[j, c]
+
         parts = [new(f"parts{j}", [P, CHUNKS], F32) for j in range(TILES)]
         norm = [new(f"norm{j}", [P, 4], F32) for j in range(TILES)]
         curve = [new(f"curve{j}", [P, 3], F32) for j in range(TILES)]
@@ -143,7 +159,7 @@ def tile_hgcn_pb_kernel(tc, x, w_sp, out):
 
         def square(j, c):
             squares = waste.tile([P, BANK], F32, name="squares")
-            nc.scalar.activation(out=squares[:], in_=sums[j, c][:], func=ACT.Square, accum_out=parts[j][:, c : c + 1])
+            nc.scalar.activation(out=squares[:], in_=to_square[j, c][:], func=ACT.Square, accum_out=parts[j][:, c : c + 1])
 
         def partial_sum(j):
             nc.gpsimd.tensor_scalar(
@@ -186,12 +202,12 @@ def tile_hgcn_pb_kernel(tc, x, w_sp, out):
 
         def scale_vector(j, c):
             nc.vector.tensor_scalar(
-                out=spatial(j, c), in0=sums[j, c][:], scalar1=factor[j][:, 1:2], scalar2=factor[j][:, 2:3],
+                out=spatial(j, c), in0=to_scale[j, c][:], scalar1=factor[j][:, 1:2], scalar2=factor[j][:, 2:3],
                 op0=ALU.mult, op1=ALU.mult,
             )
 
         def scale_scalar(j, c):
-            nc.scalar.activation(out=spatial(j, c), in_=sums[j, c][:], func=ACT.Copy, scale=factor[j][:, 3:4])
+            nc.scalar.activation(out=spatial(j, c), in_=to_scale[j, c][:], func=ACT.Copy, scale=factor[j][:, 3:4])
 
         def store(j, c_lo, c_hi):
             lo = j * D + c_lo * BANK
@@ -200,72 +216,85 @@ def tile_hgcn_pb_kernel(tc, x, w_sp, out):
                 hi = TILES * ROW
             nc.sync.dma_start(out=out_rows[:, lo:hi], in_=result[:, lo:hi])
 
-        interleave_vector(0)
-        interleave_scalar(0)
-        interleave_vector(1)
-        quantize_w(0)
-        interleave_scalar(1)
+        square_order = [(j, c) for c in range(CHUNKS) for j in range(PAIR)]
+        square_order[5], square_order[6] = square_order[6], square_order[5]
+        square_order += [(j, c) for j in range(PAIR, TILES) for c in range(CHUNKS)]
         transpose_x(0)
         unload_x(nc.scalar.copy, 0)
+        interleave(nc.vector.tensor_copy, 0, 0, BANK // 2)
+        interleave(nc.vector.tensor_copy, 0, BANK // 2, BANK)
+        quantize_x(0)
+        quantize_w(0)
+        interleave(nc.scalar.copy, 1, 0, BANK // 2)
+        interleave(nc.scalar.copy, 1, BANK // 2, BANK)
+        multiply(to_square, 0, 0)
+        multiply(to_square, 1, 0)
         interleave_vector(2)
         quantize_w(1)
-        quantize_x(0)
+        multiply(to_square, 0, 1)
+        multiply(to_square, 1, 1)
+        square(0, 0)
+        square(1, 0)
         interleave_scalar(2)
         interleave_vector(3)
         quantize_w(2)
-        quantize_w(3)
-        for c in range(CHUNKS - 1):
-            multiply(0, c)
-            square(0, c)
-        partial_sum(0)
-        multiply(1, 0)
         transpose_x(1)
-        multiply(0, CHUNKS - 1)
-        square(0, CHUNKS - 1)
-        radius(0)
-        for g in range(2, pairs):
-            transpose_x(g)
-        for g in range(1, pairs):
-            unload_x(nc.vector.tensor_copy, g)
-            multiply(1, g)
-        for g in range(1, pairs):
-            quantize_x(g)
+        transpose_x(2)
+        multiply(to_square, 0, 2)
+        quantize_w(3)
+        multiply(to_square, 0, 3)
+        unload_x(nc.vector.tensor_copy, 1)
+        step_square(2)
+        step_square(3)
+        transpose_x(3)
+        unload_x(nc.vector.tensor_copy, 2)
+        quantize_x(1)
+        unload_x(nc.vector.tensor_copy, 3)
+        quantize_x(2)
+        quantize_x(3)
+        for n in range(4, 8):
+            step_square(n)
+            multiply(to_scale, 0, n - 4)
+        hyperbolics(0)
+        invert_radius(0)
+        make_sinh(0)
 
         last = TILES - 1
-        for j in range(TILES):
-            if j < last:
-                square(j + 1, 0)
-                square(j + 1, 1)
-            else:
-                scale_scalar(j - 1, CHUNKS - 1)
-                store(j - 1, 2, CHUNKS)
-            invert_radius(j)
-            hyperbolics(j)
-            make_sinh(j)
-            if j == last:
-                make_factor(j)
-                for c in range(2):
-                    scale_vector(j, c)
-                    scale_scalar(j, c + 2)
-                    store(j, c, c + 1)
-                store(j, 2, 3)
-                store(j, 3, 4)
-                continue
+        step_square(8)
+        n = 9
+        for j in range(last - 1):
             for c in range(CHUNKS):
-                if c == 0:
-                    square(j + 1, 2)
-                    partial_sum(j + 1)
-                if c == 1:
-                    square(j + 1, 3)
-                    radius(j + 1)
-                if (j, c) == (last - 1, CHUNKS - 1):
-                    continue
+                if n < len(square_order):
+                    step_square(n)
+                    n += 1
+                if c == HYP:
+                    hyperbolics(j + 1)
+                if c == CHUNKS - 1:
+                    invert_radius(j + 1)
+                    make_sinh(j + 1)
+                    if j + 1 == last - 1:
+                        make_factor(j + 1)
                 scale_vector(j, c)
-                if (j, c) == (last - 1, 0):
-                    make_factor(j)
-                if j + 2 < TILES:
-                    multiply(j + 2, c)
+                multiply(to_scale, j + 1, c)
                 if j == 0:
                     store(j, c, c + 1)
                 elif c % 2 == 1:
                     store(j, c - 1, c + 1)
+        j = last - 1
+        scale_scalar(j, 1)
+        scale_vector(j, 0)
+        store(j, 0, 2)
+        scale_vector(j, 2)
+        scale_vector(j, 3)
+        store(j, 2, 4)
+        hyperbolics(last)
+        invert_radius(last)
+        make_sinh(last)
+        make_factor(last)
+        for c in range(CHUNKS):
+            hold(last, c)
+        for c in range(0, CHUNKS, 2):
+            scale_vector(last, c)
+            scale_scalar(last, c + 1)
+            store(last, c, c + 1)
+            store(last, c + 1, c + 2)

@@ -26,9 +26,9 @@ CHUNKS = D // BANK
 ROW = D + 1
 PAIR = 2
 RUN = 4
-SCALAR_COLS = (0, 512, 128, 0)
+SCALAR_COLS = (0, 384, 128, 128)
 ROTATE = 1
-HYP = 1
+HYP = 2
 
 
 def tile_hgcn_pb_kernel(tc, x, w_sp, out):
@@ -39,7 +39,7 @@ def tile_hgcn_pb_kernel(tc, x, w_sp, out):
 
     with ExitStack() as ctx:
         keep = ctx.enter_context(tc.tile_pool(name="keep", bufs=1))
-        waste = ctx.enter_context(tc.tile_pool(name="waste", bufs=4))
+        waste = ctx.enter_context(tc.tile_pool(name="waste", bufs=TILES * CHUNKS))
         psum = ctx.enter_context(tc.psum_pool(name="psum", bufs=CHUNKS))
         ctx.enter_context(tc.manual_schedule())
 
@@ -99,10 +99,6 @@ def tile_hgcn_pb_kernel(tc, x, w_sp, out):
             square(j, c)
             if n + CHUNKS < len(square_order):
                 multiply(to_square, *square_order[n + CHUNKS])
-            if c == CHUNKS - 2:
-                partial_sum(j)
-            if c == CHUNKS - 1:
-                radius(j)
 
         def quantize_w(c):
             nc.vector.quantize_mx(
@@ -153,7 +149,8 @@ def tile_hgcn_pb_kernel(tc, x, w_sp, out):
             to_scale[j, c] = to_square[j, c]
 
         parts = [new(f"parts{j}", [P, CHUNKS], F32) for j in range(TILES)]
-        norm = [new(f"norm{j}", [P, 4], F32) for j in range(TILES)]
+        total = [new(f"total{j}", [P, 1], F32) for j in range(TILES)]
+        radius = [new(f"radius{j}", [P, 1], F32) for j in range(TILES)]
         curve = [new(f"curve{j}", [P, 3], F32) for j in range(TILES)]
         factor = [new(f"factor{j}", [P, 4], F32) for j in range(TILES)]
 
@@ -161,31 +158,25 @@ def tile_hgcn_pb_kernel(tc, x, w_sp, out):
             squares = waste.tile([P, BANK], F32, name="squares")
             nc.scalar.activation(out=squares[:], in_=to_square[j, c][:], func=ACT.Square, accum_out=parts[j][:, c : c + 1])
 
-        def partial_sum(j):
-            nc.gpsimd.tensor_scalar(
-                out=norm[j][:, 0:1], in0=parts[j][:, 0:1], scalar1=parts[j][:, 1:2], scalar2=parts[j][:, 2:3],
-                op0=ALU.add, op1=ALU.add,
-            )
+        def add_parts(j):
+            nc.vector.tensor_reduce(out=total[j][:], in_=parts[j][:], axis=mybir.AxisListType.X, op=ALU.add)
+            nc.gpsimd.tensor_tensor(out=radius[j][:], in0=total[j][:], in1=half[:], op=ALU.pow)
 
-        def radius(j):
-            nc.gpsimd.tensor_tensor(out=norm[j][:, 1:2], in0=parts[j][:, 3:4], in1=norm[j][:, 0:1], op=ALU.add)
-            nc.gpsimd.tensor_tensor(out=norm[j][:, 2:3], in0=norm[j][:, 1:2], in1=half[:], op=ALU.pow)
-            nc.gpsimd.tensor_scalar(
-                out=norm[j][:, 3:4], in0=norm[j][:, 2:3], scalar1=EPS, scalar2=None, op0=ALU.max
-            )
+        def clamp_radius(j):
+            nc.vector.tensor_scalar(out=factor[j][:, 0:1], in0=radius[j][:], scalar1=EPS, scalar2=None, op0=ALU.max)
 
         def time_coordinate(j):
             return result[:, j * ROW : j * ROW + 1]
 
         def hyperbolics(j):
-            r = norm[j][:, 2:3]
+            r = radius[j][:]
             nc.scalar.activation(
                 out=curve[j][:, 0:2], in_=signs[:], func=ACT.Exp, scale=r, bias=neg_ln2[:], accum_out=time_coordinate(j)
             )
             nc.scalar.activation(out=curve[j][:, 2:3], in_=r, func=ACT.Tanh)
 
         def invert_radius(j):
-            nc.vector.reciprocal(out=factor[j][:, 1:2], in_=norm[j][:, 3:4])
+            nc.vector.reciprocal(out=factor[j][:, 1:2], in_=factor[j][:, 0:1])
 
         def make_sinh(j):
             nc.vector.tensor_scalar(
@@ -225,42 +216,52 @@ def tile_hgcn_pb_kernel(tc, x, w_sp, out):
         interleave(nc.vector.tensor_copy, 0, BANK // 2, BANK)
         quantize_x(0)
         quantize_w(0)
-        interleave(nc.scalar.copy, 1, 0, BANK // 2)
+        interleave(nc.scalar.copy, 1, BANK - SCALAR_COLS[1], BANK // 2)
         interleave(nc.scalar.copy, 1, BANK // 2, BANK)
         multiply(to_square, 0, 0)
         multiply(to_square, 1, 0)
+        interleave_vector(1)
         interleave_vector(2)
+        interleave_scalar(2)
         quantize_w(1)
         multiply(to_square, 0, 1)
         multiply(to_square, 1, 1)
         square(0, 0)
         square(1, 0)
-        interleave_scalar(2)
+        interleave_scalar(3)
         interleave_vector(3)
         quantize_w(2)
         transpose_x(1)
-        transpose_x(2)
         multiply(to_square, 0, 2)
         quantize_w(3)
         multiply(to_square, 0, 3)
         unload_x(nc.vector.tensor_copy, 1)
         step_square(2)
         step_square(3)
+        transpose_x(2)
         transpose_x(3)
-        unload_x(nc.vector.tensor_copy, 2)
         quantize_x(1)
+        step_square(4)
+        step_square(5)
+        add_parts(0)
+        unload_x(nc.vector.tensor_copy, 2)
         unload_x(nc.vector.tensor_copy, 3)
+        multiply(to_scale, 0, 0)
+        step_square(6)
+        multiply(to_scale, 0, 1)
+        step_square(7)
+        multiply(to_scale, 0, 2)
+        step_square(8)
+        multiply(to_scale, 0, 3)
+        clamp_radius(0)
         quantize_x(2)
-        quantize_x(3)
-        for n in range(4, 8):
-            step_square(n)
-            multiply(to_scale, 0, n - 4)
-        hyperbolics(0)
         invert_radius(0)
+        quantize_x(3)
+        hyperbolics(0)
         make_sinh(0)
+        add_parts(1)
 
         last = TILES - 1
-        step_square(8)
         n = 9
         for j in range(last - 1):
             for c in range(CHUNKS):
@@ -269,25 +270,35 @@ def tile_hgcn_pb_kernel(tc, x, w_sp, out):
                     n += 1
                 if c == HYP:
                     hyperbolics(j + 1)
-                if c == CHUNKS - 1:
+                if c == 2:
+                    clamp_radius(j + 1)
+                if c == 3:
                     invert_radius(j + 1)
                     make_sinh(j + 1)
-                    if j + 1 == last - 1:
-                        make_factor(j + 1)
-                scale_vector(j, c)
+                    add_parts(j + 2)
+                if c == 0 and j == last - 2:
+                    make_factor(j)
+                if (j, c) == (last - 2, CHUNKS - 1):
+                    scale_scalar(j, c)
+                else:
+                    scale_vector(j, c)
                 multiply(to_scale, j + 1, c)
-                if j == 0:
+                if j == 0 or j == last - 2:
                     store(j, c, c + 1)
                 elif c % 2 == 1:
                     store(j, c - 1, c + 1)
         j = last - 1
-        scale_scalar(j, 1)
         scale_vector(j, 0)
-        store(j, 0, 2)
-        scale_vector(j, 2)
-        scale_vector(j, 3)
-        store(j, 2, 4)
+        store(j, 0, 1)
+        make_factor(j)
+        scale_vector(j, 1)
+        store(j, 1, 2)
+        clamp_radius(last)
         hyperbolics(last)
+        scale_vector(j, 2)
+        store(j, 2, 3)
+        scale_scalar(j, 3)
+        store(j, 3, 4)
         invert_radius(last)
         make_sinh(last)
         make_factor(last)

@@ -22,13 +22,17 @@ P = 128
 PACK = 4
 TILES = B * N // P
 BANK = 512
+HALF = BANK // 2
 CHUNKS = D // BANK
 ROW = D + 1
 PAIR = 2
+PAIRS = TILES // PAIR
 RUN = 4
-SCALAR_COLS = (0, 384, 128, 128)
-ROTATE = 1
-HYP = 2
+LAST = TILES - 1
+
+SCALAR_COLS = {1: 384, 2: 128, 3: 128}
+FIRST_STORE_CHUNKS = 1
+STORE_CHUNKS = 2
 
 
 def tile_hgcn_pb_kernel(tc, x, w_sp, out):
@@ -50,18 +54,17 @@ def tile_hgcn_pb_kernel(tc, x, w_sp, out):
         w_grouped = [new(f"w_grouped{c}", [P, BANK, PACK], BF16) for c in range(CHUNKS)]
         w_codes = [new(f"w_codes{c}", [P, BANK], U32) for c in range(CHUNKS)]
         w_scales = [new(f"w_scales{c}", [P, BANK], U8) for c in range(CHUNKS)]
-        pairs = TILES // PAIR
-        x_raw = [new(f"x_raw{g}", [P, PAIR, F], BF16) for g in range(pairs)]
-        x_grouped = [new(f"x_grouped{g}", [P, PAIR * P * PACK], BF16) for g in range(pairs)]
-        x_codes = [new(f"x_codes{g}", [P, PAIR * P], U32) for g in range(pairs)]
-        x_scales = [new(f"x_scales{g}", [P, PAIR * P], U8) for g in range(pairs)]
+        x_raw = [new(f"x_raw{g}", [P, PAIR, F], BF16) for g in range(PAIRS)]
+        x_grouped = [new(f"x_grouped{g}", [P, PAIR * P * PACK], BF16) for g in range(PAIRS)]
+        x_codes = [new(f"x_codes{g}", [P, PAIR * P], U32) for g in range(PAIRS)]
+        x_scales = [new(f"x_scales{g}", [P, PAIR * P], U8) for g in range(PAIRS)]
         result = new("result", [P, TILES * ROW], F32)
         identity = new("identity", [P, P], F32)
         signs = new("signs", [P, 2], F32)
-        half = new("half", [P, 1], F32)
+        root_power = new("root_power", [P, 1], F32)
         neg_ln2 = new("neg_ln2", [P, 1], F32)
 
-        def load_w(c, lo=0, hi=BANK):
+        def load_w(c, lo, hi):
             nc.sync.dma_start(out=w_raw[c][:, :, lo:hi], in_=w_rows[:, :, c * BANK + lo : c * BANK + hi])
 
         def load_x(g):
@@ -69,18 +72,19 @@ def tile_hgcn_pb_kernel(tc, x, w_sp, out):
 
         load_x(0)
         for c in range(2):
-            load_w(c, 0, BANK // 2)
-            load_w(c, BANK // 2, BANK)
+            load_w(c, 0, HALF)
+            load_w(c, HALF, BANK)
         for c in range(2, CHUNKS):
-            load_w(c)
-        for g in range(1, pairs):
+            load_w(c, 0, BANK)
+        for g in range(1, PAIRS):
             load_x(g)
 
         nc.gpsimd.memset(signs[:, 0:1], 1.0)
         nc.gpsimd.memset(signs[:, 1:2], -1.0)
-        nc.gpsimd.memset(half[:], 0.5)
+        nc.gpsimd.memset(root_power[:], 0.5)
         make_identity(nc, identity[:])
         nc.scalar.activation(out=neg_ln2[:], in_=signs[:, 1:2], func=ACT.Identity, scale=math.log(2.0))
+
 
         def interleave(copy, c, lo, hi):
             copy(
@@ -94,18 +98,13 @@ def tile_hgcn_pb_kernel(tc, x, w_sp, out):
         def interleave_vector(c):
             interleave(nc.vector.tensor_copy, c, 0, BANK - SCALAR_COLS[c])
 
-        def step_square(n):
-            j, c = square_order[n]
-            square(j, c)
-            if n + CHUNKS < len(square_order):
-                multiply(to_square, *square_order[n + CHUNKS])
-
         def quantize_w(c):
             nc.vector.quantize_mx(
                 out=w_codes[c][:].bitcast(E4M3X4),
                 scales=w_scales[c][:],
                 in_=w_grouped[c][:].rearrange("p n t -> p (n t)"),
             )
+
 
         x_banks = {}
 
@@ -116,7 +115,7 @@ def tile_hgcn_pb_kernel(tc, x, w_sp, out):
                 words = x_raw[g][:, i, :].bitcast(F32)
                 for u in range(2):
                     at = (2 * i + u) * P
-                    nc.tensor.transpose(bank[:, at : at + P], words[:, u :: 2], identity[:])
+                    nc.tensor.transpose(bank[:, at : at + P], words[:, u::2], identity[:])
 
         def unload_x(copy, g):
             copy(
@@ -127,12 +126,13 @@ def tile_hgcn_pb_kernel(tc, x, w_sp, out):
         def quantize_x(g):
             nc.vector.quantize_mx(out=x_codes[g][:].bitcast(E5M2X4), scales=x_scales[g][:], in_=x_grouped[g][:])
 
+
         to_square, to_scale = {}, {}
 
-        def multiply(sums, j, c):
-            tag = "square_banks" if sums is to_square else "scale_banks"
+        def multiply(banks, j, c):
+            tag = "square_banks" if banks is to_square else "scale_banks"
             bank = psum.tile([P, BANK], F32, name=f"{tag}_{j}_{c}", tag=tag)
-            sums[j, c] = bank
+            banks[j, c] = bank
             g, i = divmod(j, PAIR)
             tokens = slice(i * P, (i + 1) * P)
             nc.tensor.matmul_mx(
@@ -145,8 +145,6 @@ def tile_hgcn_pb_kernel(tc, x, w_sp, out):
                 stop=True,
             )
 
-        def hold(j, c):
-            to_scale[j, c] = to_square[j, c]
 
         parts = [new(f"parts{j}", [P, CHUNKS], F32) for j in range(TILES)]
         total = [new(f"total{j}", [P, 1], F32) for j in range(TILES)]
@@ -156,11 +154,13 @@ def tile_hgcn_pb_kernel(tc, x, w_sp, out):
 
         def square(j, c):
             squares = waste.tile([P, BANK], F32, name="squares")
-            nc.scalar.activation(out=squares[:], in_=to_square[j, c][:], func=ACT.Square, accum_out=parts[j][:, c : c + 1])
+            nc.scalar.activation(
+                out=squares[:], in_=to_square[j, c][:], func=ACT.Square, accum_out=parts[j][:, c : c + 1]
+            )
 
-        def add_parts(j):
+        def find_radius(j):
             nc.vector.tensor_reduce(out=total[j][:], in_=parts[j][:], axis=mybir.AxisListType.X, op=ALU.add)
-            nc.gpsimd.tensor_tensor(out=radius[j][:], in0=total[j][:], in1=half[:], op=ALU.pow)
+            nc.gpsimd.tensor_tensor(out=radius[j][:], in0=total[j][:], in1=root_power[:], op=ALU.pow)
 
         def clamp_radius(j):
             nc.vector.tensor_scalar(out=factor[j][:, 0:1], in0=radius[j][:], scalar1=EPS, scalar2=None, op0=ALU.max)
@@ -187,6 +187,7 @@ def tile_hgcn_pb_kernel(tc, x, w_sp, out):
         def make_factor(j):
             nc.vector.tensor_tensor(out=factor[j][:, 3:4], in0=factor[j][:, 1:2], in1=factor[j][:, 2:3], op=ALU.mult)
 
+
         def spatial(j, c):
             at = j * ROW + 1 + c * BANK
             return result[:, at : at + BANK]
@@ -200,24 +201,30 @@ def tile_hgcn_pb_kernel(tc, x, w_sp, out):
         def scale_scalar(j, c):
             nc.scalar.activation(out=spatial(j, c), in_=to_scale[j, c][:], func=ACT.Copy, scale=factor[j][:, 3:4])
 
-        def store(j, c_lo, c_hi):
-            lo = j * D + c_lo * BANK
-            hi = j * D + c_hi * BANK
-            if (j, c_hi) == (TILES - 1, CHUNKS):
-                hi = TILES * ROW
-            nc.sync.dma_start(out=out_rows[:, lo:hi], in_=result[:, lo:hi])
+        def store_after(j, c):
+            chunks = FIRST_STORE_CHUNKS if j == 0 else STORE_CHUNKS
+            if (c + 1) % chunks == 0:
+                lo = j * D + (c + 1 - chunks) * BANK
+                hi = TILES * ROW if (j, c) == (LAST, CHUNKS - 1) else j * D + (c + 1) * BANK
+                nc.sync.dma_start(out=out_rows[:, lo:hi], in_=result[:, lo:hi])
 
-        square_order = [(j, c) for c in range(CHUNKS) for j in range(PAIR)]
-        square_order[5], square_order[6] = square_order[6], square_order[5]
+        square_order = [(j, c) for c in range(2) for j in range(PAIR)]
+        square_order += [(j, c) for j in range(PAIR) for c in range(2, CHUNKS)]
         square_order += [(j, c) for j in range(PAIR, TILES) for c in range(CHUNKS)]
+
+        def square_step(n):
+            square(*square_order[n])
+            if n + CHUNKS < len(square_order):
+                multiply(to_square, *square_order[n + CHUNKS])
+
         transpose_x(0)
         unload_x(nc.scalar.copy, 0)
-        interleave(nc.vector.tensor_copy, 0, 0, BANK // 2)
-        interleave(nc.vector.tensor_copy, 0, BANK // 2, BANK)
+        interleave(nc.vector.tensor_copy, 0, 0, HALF)
+        interleave(nc.vector.tensor_copy, 0, HALF, BANK)
         quantize_x(0)
         quantize_w(0)
-        interleave(nc.scalar.copy, 1, BANK - SCALAR_COLS[1], BANK // 2)
-        interleave(nc.scalar.copy, 1, BANK // 2, BANK)
+        interleave(nc.scalar.copy, 1, BANK - SCALAR_COLS[1], HALF)
+        interleave(nc.scalar.copy, 1, HALF, BANK)
         multiply(to_square, 0, 0)
         multiply(to_square, 1, 0)
         interleave_vector(1)
@@ -235,77 +242,67 @@ def tile_hgcn_pb_kernel(tc, x, w_sp, out):
         multiply(to_square, 0, 2)
         quantize_w(3)
         multiply(to_square, 0, 3)
+
         unload_x(nc.vector.tensor_copy, 1)
-        step_square(2)
-        step_square(3)
+        square_step(2)
+        square_step(3)
         transpose_x(2)
         transpose_x(3)
         quantize_x(1)
-        step_square(4)
-        step_square(5)
-        add_parts(0)
+        square_step(4)
+        square_step(5)
+        find_radius(0)
         unload_x(nc.vector.tensor_copy, 2)
         unload_x(nc.vector.tensor_copy, 3)
         multiply(to_scale, 0, 0)
-        step_square(6)
-        multiply(to_scale, 0, 1)
-        step_square(7)
-        multiply(to_scale, 0, 2)
-        step_square(8)
-        multiply(to_scale, 0, 3)
+        for c in range(1, CHUNKS):
+            square_step(5 + c)
+            multiply(to_scale, 0, c)
         clamp_radius(0)
         quantize_x(2)
         invert_radius(0)
         quantize_x(3)
         hyperbolics(0)
         make_sinh(0)
-        add_parts(1)
+        find_radius(1)
 
-        last = TILES - 1
-        n = 9
-        for j in range(last - 1):
+        for j in range(LAST - 1):
             for c in range(CHUNKS):
+                n = (j + 2) * CHUNKS + c + 1
                 if n < len(square_order):
-                    step_square(n)
-                    n += 1
-                if c == HYP:
+                    square_step(n)
+                if c == CHUNKS - 2:
                     hyperbolics(j + 1)
-                if c == 2:
                     clamp_radius(j + 1)
-                if c == 3:
+                if c == CHUNKS - 1:
                     invert_radius(j + 1)
                     make_sinh(j + 1)
-                    add_parts(j + 2)
-                if c == 0 and j == last - 2:
+                    find_radius(j + 2)
+                if (j, c) == (LAST - 2, 0):
                     make_factor(j)
-                if (j, c) == (last - 2, CHUNKS - 1):
+                if (j, c) == (LAST - 2, CHUNKS - 1):
                     scale_scalar(j, c)
                 else:
                     scale_vector(j, c)
                 multiply(to_scale, j + 1, c)
-                if j == 0 or j == last - 2:
-                    store(j, c, c + 1)
-                elif c % 2 == 1:
-                    store(j, c - 1, c + 1)
-        j = last - 1
+                store_after(j, c)
+
+        j = LAST - 1
         scale_vector(j, 0)
-        store(j, 0, 1)
         make_factor(j)
         scale_vector(j, 1)
-        store(j, 1, 2)
-        clamp_radius(last)
-        hyperbolics(last)
+        store_after(j, 1)
+        clamp_radius(LAST)
+        hyperbolics(LAST)
         scale_vector(j, 2)
-        store(j, 2, 3)
         scale_scalar(j, 3)
-        store(j, 3, 4)
-        invert_radius(last)
-        make_sinh(last)
-        make_factor(last)
+        store_after(j, 3)
+        invert_radius(LAST)
+        make_sinh(LAST)
+        make_factor(LAST)
         for c in range(CHUNKS):
-            hold(last, c)
+            to_scale[LAST, c] = to_square[LAST, c]
         for c in range(0, CHUNKS, 2):
-            scale_vector(last, c)
-            scale_scalar(last, c + 1)
-            store(last, c, c + 1)
-            store(last, c + 1, c + 2)
+            scale_vector(LAST, c)
+            scale_scalar(LAST, c + 1)
+            store_after(LAST, c + 1)

import math
from contextlib import ExitStack

import concourse.mybir as mybir
from concourse.masks import make_identity

B, N, F, D = 2, 512, 512, 2048
EPS = 1e-6
SINH_EPS = EPS + EPS**3 / 6
FLOPS = 2 * B * N * F * D

F32 = mybir.dt.float32
BF16 = mybir.dt.bfloat16
U32 = mybir.dt.uint32
U8 = mybir.dt.uint8
E5M2X4 = mybir.dt.float8_e5m2_x4
E4M3X4 = mybir.dt.float8_e4m3fn_x4
ALU = mybir.AluOpType
ACT = mybir.ActivationFunctionType

P = 128
PACK = 4
TILES = B * N // P
BANK = 512
HALF = BANK // 2
CHUNKS = D // BANK
ROW = D + 1
PAIR = 2
PAIRS = TILES // PAIR
RUN = 4
LAST = TILES - 1

SCALAR_COLS = {1: 384, 2: 128, 3: 128}
FIRST_STORE_CHUNKS = 1
STORE_CHUNKS = 2


def tile_hgcn_pb_kernel(tc, x, w_sp, out):
    nc = tc.nc
    x_rows = x.rearrange("b (q j) f -> (b q) j f", j=TILES)
    w_rows = w_sp.rearrange("(p t) d -> p t d", t=PACK)
    out_rows = out.rearrange("b (q j) d -> (b q) (j d)", j=TILES)

    with ExitStack() as ctx:
        keep = ctx.enter_context(tc.tile_pool(name="keep", bufs=1))
        waste = ctx.enter_context(tc.tile_pool(name="waste", bufs=TILES * CHUNKS))
        psum = ctx.enter_context(tc.psum_pool(name="psum", bufs=CHUNKS))
        ctx.enter_context(tc.manual_schedule())

        def new(name, shape, dtype):
            return keep.tile(shape, dtype, name=name, align_bytes=64)

        w_raw = [new(f"w_raw{c}", [P, PACK, BANK], BF16) for c in range(CHUNKS)]
        w_grouped = [new(f"w_grouped{c}", [P, BANK, PACK], BF16) for c in range(CHUNKS)]
        w_codes = [new(f"w_codes{c}", [P, BANK], U32) for c in range(CHUNKS)]
        w_scales = [new(f"w_scales{c}", [P, BANK], U8) for c in range(CHUNKS)]
        x_raw = [new(f"x_raw{g}", [P, PAIR, F], BF16) for g in range(PAIRS)]
        x_grouped = [new(f"x_grouped{g}", [P, PAIR * P * PACK], BF16) for g in range(PAIRS)]
        x_codes = [new(f"x_codes{g}", [P, PAIR * P], U32) for g in range(PAIRS)]
        x_scales = [new(f"x_scales{g}", [P, PAIR * P], U8) for g in range(PAIRS)]
        result = new("result", [P, TILES * ROW], F32)
        identity = new("identity", [P, P], F32)
        signs = new("signs", [P, 2], F32)
        root_power = new("root_power", [P, 1], F32)
        neg_ln2 = new("neg_ln2", [P, 1], F32)

        def load_w(c, lo, hi):
            nc.sync.dma_start(out=w_raw[c][:, :, lo:hi], in_=w_rows[:, :, c * BANK + lo : c * BANK + hi])

        def load_x(g):
            nc.sync.dma_start(out=x_raw[g][:], in_=x_rows[:, g * PAIR : (g + 1) * PAIR, :])

        load_x(0)
        for c in range(2):
            load_w(c, 0, HALF)
            load_w(c, HALF, BANK)
        for c in range(2, CHUNKS):
            load_w(c, 0, BANK)
        for g in range(1, PAIRS):
            load_x(g)

        nc.gpsimd.memset(signs[:, 0:1], 1.0)
        nc.gpsimd.memset(signs[:, 1:2], -1.0)
        nc.gpsimd.memset(root_power[:], 0.5)
        make_identity(nc, identity[:])
        nc.scalar.activation(out=neg_ln2[:], in_=signs[:, 1:2], func=ACT.Identity, scale=math.log(2.0))


        def interleave(copy, c, lo, hi):
            copy(
                out=w_grouped[c][:, lo:hi, :].rearrange("p (n i) t -> p n t i", i=RUN),
                in_=w_raw[c][:, :, lo:hi].rearrange("p t (n i) -> p n t i", i=RUN),
            )

        def interleave_scalar(c):
            interleave(nc.scalar.copy, c, BANK - SCALAR_COLS[c], BANK)

        def interleave_vector(c):
            interleave(nc.vector.tensor_copy, c, 0, BANK - SCALAR_COLS[c])

        def quantize_w(c):
            nc.vector.quantize_mx(
                out=w_codes[c][:].bitcast(E4M3X4),
                scales=w_scales[c][:],
                in_=w_grouped[c][:].rearrange("p n t -> p (n t)"),
            )


        x_banks = {}

        def transpose_x(g):
            bank = psum.tile([P, BANK], F32, name=f"x_bank{g}", tag="scale_banks")
            x_banks[g] = bank
            for i in range(PAIR):
                words = x_raw[g][:, i, :].bitcast(F32)
                for u in range(2):
                    at = (2 * i + u) * P
                    nc.tensor.transpose(bank[:, at : at + P], words[:, u::2], identity[:])

        def unload_x(copy, g):
            copy(
                out=x_grouped[g][:].bitcast(F32).rearrange("p (i r u) -> p i r u", i=PAIR, u=2),
                in_=x_banks[g][:].rearrange("p (i u r) -> p i r u", i=PAIR, u=2),
            )

        def quantize_x(g):
            nc.vector.quantize_mx(out=x_codes[g][:].bitcast(E5M2X4), scales=x_scales[g][:], in_=x_grouped[g][:])


        to_square, to_scale = {}, {}

        def multiply(banks, j, c):
            tag = "square_banks" if banks is to_square else "scale_banks"
            bank = psum.tile([P, BANK], F32, name=f"{tag}_{j}_{c}", tag=tag)
            banks[j, c] = bank
            g, i = divmod(j, PAIR)
            tokens = slice(i * P, (i + 1) * P)
            nc.tensor.matmul_mx(
                out=bank[:],
                lhsT=x_codes[g][:, tokens].bitcast(E5M2X4),
                lhsT_scale=x_scales[g][:, tokens],
                rhs=w_codes[c][:].bitcast(E4M3X4),
                rhs_scale=w_scales[c][:],
                start=True,
                stop=True,
            )


        parts = [new(f"parts{j}", [P, CHUNKS], F32) for j in range(TILES)]
        total = [new(f"total{j}", [P, 1], F32) for j in range(TILES)]
        radius = [new(f"radius{j}", [P, 1], F32) for j in range(TILES)]
        curve = [new(f"curve{j}", [P, 3], F32) for j in range(TILES)]
        factor = [new(f"factor{j}", [P, 4], F32) for j in range(TILES)]

        def square(j, c):
            squares = waste.tile([P, BANK], F32, name="squares")
            nc.scalar.activation(
                out=squares[:], in_=to_square[j, c][:], func=ACT.Square, accum_out=parts[j][:, c : c + 1]
            )

        def find_radius(j):
            nc.vector.tensor_reduce(out=total[j][:], in_=parts[j][:], axis=mybir.AxisListType.X, op=ALU.add)
            nc.gpsimd.tensor_tensor(out=radius[j][:], in0=total[j][:], in1=root_power[:], op=ALU.pow)

        def clamp_radius(j):
            nc.vector.tensor_scalar(out=factor[j][:, 0:1], in0=radius[j][:], scalar1=EPS, scalar2=None, op0=ALU.max)

        def time_coordinate(j):
            return result[:, j * ROW : j * ROW + 1]

        def hyperbolics(j):
            r = radius[j][:]
            nc.scalar.activation(
                out=curve[j][:, 0:2], in_=signs[:], func=ACT.Exp, scale=r, bias=neg_ln2[:], accum_out=time_coordinate(j)
            )
            nc.scalar.activation(out=curve[j][:, 2:3], in_=r, func=ACT.Tanh)

        def invert_radius(j):
            nc.vector.reciprocal(out=factor[j][:, 1:2], in_=factor[j][:, 0:1])

        def make_sinh(j):
            nc.vector.tensor_scalar(
                out=factor[j][:, 2:3], in0=curve[j][:, 2:3], scalar1=time_coordinate(j), scalar2=SINH_EPS,
                op0=ALU.mult, op1=ALU.max,
            )

        def make_factor(j):
            nc.vector.tensor_tensor(out=factor[j][:, 3:4], in0=factor[j][:, 1:2], in1=factor[j][:, 2:3], op=ALU.mult)


        def spatial(j, c):
            at = j * ROW + 1 + c * BANK
            return result[:, at : at + BANK]

        def scale_vector(j, c):
            nc.vector.tensor_scalar(
                out=spatial(j, c), in0=to_scale[j, c][:], scalar1=factor[j][:, 1:2], scalar2=factor[j][:, 2:3],
                op0=ALU.mult, op1=ALU.mult,
            )

        def scale_scalar(j, c):
            nc.scalar.activation(out=spatial(j, c), in_=to_scale[j, c][:], func=ACT.Copy, scale=factor[j][:, 3:4])

        def store_after(j, c):
            chunks = FIRST_STORE_CHUNKS if j == 0 else STORE_CHUNKS
            if (c + 1) % chunks == 0:
                lo = j * D + (c + 1 - chunks) * BANK
                hi = TILES * ROW if (j, c) == (LAST, CHUNKS - 1) else j * D + (c + 1) * BANK
                nc.sync.dma_start(out=out_rows[:, lo:hi], in_=result[:, lo:hi])

        square_order = [(j, c) for c in range(2) for j in range(PAIR)]
        square_order += [(j, c) for j in range(PAIR) for c in range(2, CHUNKS)]
        square_order += [(j, c) for j in range(PAIR, TILES) for c in range(CHUNKS)]

        def square_step(n):
            square(*square_order[n])
            if n + CHUNKS < len(square_order):
                multiply(to_square, *square_order[n + CHUNKS])

        transpose_x(0)
        unload_x(nc.scalar.copy, 0)
        interleave(nc.vector.tensor_copy, 0, 0, HALF)
        interleave(nc.vector.tensor_copy, 0, HALF, BANK)
        quantize_x(0)
        quantize_w(0)
        interleave(nc.scalar.copy, 1, BANK - SCALAR_COLS[1], HALF)
        interleave(nc.scalar.copy, 1, HALF, BANK)
        multiply(to_square, 0, 0)
        multiply(to_square, 1, 0)
        interleave_vector(1)
        interleave_vector(2)
        interleave_scalar(2)
        quantize_w(1)
        multiply(to_square, 0, 1)
        multiply(to_square, 1, 1)
        square(0, 0)
        square(1, 0)
        interleave_scalar(3)
        interleave_vector(3)
        quantize_w(2)
        transpose_x(1)
        multiply(to_square, 0, 2)
        quantize_w(3)
        multiply(to_square, 0, 3)

        unload_x(nc.vector.tensor_copy, 1)
        square_step(2)
        square_step(3)
        transpose_x(2)
        transpose_x(3)
        quantize_x(1)
        square_step(4)
        square_step(5)
        find_radius(0)
        unload_x(nc.vector.tensor_copy, 2)
        unload_x(nc.vector.tensor_copy, 3)
        multiply(to_scale, 0, 0)
        for c in range(1, CHUNKS):
            square_step(5 + c)
            multiply(to_scale, 0, c)
        clamp_radius(0)
        quantize_x(2)
        invert_radius(0)
        quantize_x(3)
        hyperbolics(0)
        make_sinh(0)
        find_radius(1)

        for j in range(LAST - 1):
            for c in range(CHUNKS):
                n = (j + 2) * CHUNKS + c + 1
                if n < len(square_order):
                    square_step(n)
                if c == CHUNKS - 2:
                    hyperbolics(j + 1)
                    clamp_radius(j + 1)
                if c == CHUNKS - 1:
                    invert_radius(j + 1)
                    make_sinh(j + 1)
                    find_radius(j + 2)
                if (j, c) == (LAST - 2, 0):
                    make_factor(j)
                if (j, c) == (LAST - 2, CHUNKS - 1):
                    scale_scalar(j, c)
                else:
                    scale_vector(j, c)
                multiply(to_scale, j + 1, c)
                store_after(j, c)

        j = LAST - 1
        scale_vector(j, 0)
        make_factor(j)
        scale_vector(j, 1)
        store_after(j, 1)
        clamp_radius(LAST)
        hyperbolics(LAST)
        scale_vector(j, 2)
        scale_scalar(j, 3)
        store_after(j, 3)
        invert_radius(LAST)
        make_sinh(LAST)
        make_factor(LAST)
        for c in range(CHUNKS):
            to_scale[LAST, c] = to_square[LAST, c]
        for c in range(0, CHUNKS, 2):
            scale_vector(LAST, c)
            scale_scalar(LAST, c + 1)
            store_after(LAST, c + 1)
